import numpy as np
import ml_dtypes


def mxq(x, axis, fmt="e4m3"):
    dtype, down = {"e4m3": (ml_dtypes.float8_e4m3fn, 7), "e5m2": (ml_dtypes.float8_e5m2, 14)}[fmt]
    v = np.moveaxis(np.asarray(x, np.float32).astype(ml_dtypes.bfloat16).astype(np.float64), axis, -1)
    blocks = v.reshape(v.shape[:-1] + (-1, 32))
    amax = np.abs(blocks).max(-1, keepdims=True)
    byte = np.maximum(np.where(amax > 0, np.frexp(amax)[1] - 1 + 127, 0) - down, 1)
    scale = np.exp2(byte - 127.0)
    codes = (blocks / scale).astype(np.float32).astype(dtype).astype(np.float64)
    return np.moveaxis((codes * scale).reshape(v.shape), -1, axis)


WIDE = False


def mx_kscale(k, group=512):
    if not WIDE:
        return np.ones(k)
    levels = np.array([20, -20, 10, -10, 0])
    if group != 512:
        return np.exp2(np.random.permutation(np.resize(levels, k // group))).repeat(group)
    a = np.random.permutation(np.resize(levels, k // 512 * 4)).reshape(k // 512, 4)
    idx = np.arange(k)
    return np.exp2(a[idx // 512, idx % 128 // 32])


BF16 = ml_dtypes.bfloat16


def bf(x):
    return np.asarray(x, np.float32).astype(BF16)


def f64(x):
    return np.asarray(x).astype(np.float64)


N, D, C = 512, 4096, 4


def unit(v):
    return v / np.linalg.norm(v, axis=-1, keepdims=True)


def cnormal(*shape):
    return np.random.standard_normal(shape) + 1j * np.random.standard_normal(shape)


def draw_states():
    centre = unit(unit(cnormal(D)) + unit(cnormal(C, D)))
    label = np.random.randint(0, C, N)
    a2 = np.where(np.random.random(N) < 0.5, 0.95, 0.65)[:, None]
    psi = np.sqrt(a2) * centre[label] + np.sqrt(1.0 - a2) * unit(cnormal(N, D))
    theta = 2.0 * np.pi * np.random.random(N)[:, None]
    return unit(psi * np.exp(1j * theta))


def setup_inputs():
    s = mx_kscale(N, 128)
    psi = draw_states()
    r0 = bf(psi.real)
    i0 = bf(psi.imag)
    g = np.random.standard_normal((N, N)) * np.exp2(np.random.randint(-12, 1, (N, 1))) * 16.0
    g = bf(g / (s[:, None] * s[None, :]))
    rf, jf = f64(r0), f64(i0)
    g_re = rf @ rf.T + jf @ jf.T
    g_im = jf @ rf.T - rf @ jf.T
    return {"latent_re": bf(rf * s[:, None]), "latent_im": bf(jf * s[:, None]),
            "g_re": np.asarray(g_re, np.float32), "g_im": np.asarray(g_im, np.float32), "grad_out": g}


def reference(latent_re, latent_im, g_re, g_im, grad_out):
    g = f64(grad_out)
    sym = g + g.T
    p = 2.0 * sym * f64(g_re)
    q = -2.0 * sym * f64(g_im)
    a = mxq(p, 1, "e5m2") @ mxq(f64(latent_re), 0, "e4m3")
    b = mxq(q, 1, "e5m2") @ mxq(f64(latent_im), 0, "e4m3")
    return a + b

@@ -1,0 +1,157 @@
+from contextlib import ExitStack
+
+import concourse.mybir as mybir
+from concourse.masks import make_identity
+
+F32 = mybir.dt.float32
+BF16 = mybir.dt.bfloat16
+U32 = mybir.dt.uint32
+U8 = mybir.dt.uint8
+E4M3_X4 = mybir.dt.float8_e4m3fn_x4
+E5M2_X4 = mybir.dt.float8_e5m2_x4
+ADD = mybir.AluOpType.add
+MULT = mybir.AluOpType.mult
+
+P = 128
+PACK = 4
+STATES = P * PACK
+DIM = 4096
+N_TILE = 512
+LOAD_COLS = 1024
+STORE_COLS = 1024
+RUN = 4
+SCALAR_COLS = 128
+
+FLOPS = 2 * 2 * STATES * STATES * DIM
+
+
+def tile_quantumgraphneuralnetwork_pa_v_kernel(
+    tc, latent_re, latent_im, g_re, g_im, grad_out, out
+):
+    nc = tc.nc
+    with ExitStack() as stack:
+        keep = stack.enter_context(tc.tile_pool(name="keep", bufs=1))
+        stage = stack.enter_context(tc.tile_pool(name="stage", bufs=3))
+        results = stack.enter_context(tc.tile_pool(name="results", bufs=4))
+
+        grad_rows = keep.tile([P, PACK, STATES], BF16)
+        nc.sync.dma_start(out=grad_rows[:], in_=grad_out.rearrange("(p r) c -> p r c", r=PACK))
+        gram_rows = []
+        for part, gram in enumerate((g_re, g_im)):
+            rows = keep.tile([P, PACK, STATES], F32, name="gram_rows_%d" % part)
+            nc.sync.dma_start(out=rows[:], in_=gram.rearrange("(p r) c -> p r c", r=PACK))
+            gram_rows.append(rows)
+        latent_rows = [[], []]
+        for chunk in range(DIM // LOAD_COLS):
+            cols = slice(chunk * LOAD_COLS, (chunk + 1) * LOAD_COLS)
+            for part, latent in enumerate((latent_re, latent_im)):
+                rows = keep.tile([P, PACK, LOAD_COLS], BF16, name="latent_rows_%d_%d" % (part, chunk))
+                nc.sync.dma_start(
+                    out=rows[:], in_=latent.rearrange("(p t) d -> p t d", t=PACK)[:, :, cols]
+                )
+                latent_rows[part].append(rows)
+
+        ident_bf16 = keep.tile([P, P], BF16)
+        make_identity(nc, ident_bf16[:])
+        ident_f32 = keep.tile([P, P], F32)
+        make_identity(nc, ident_f32[:])
+
+        weight_codes = []
+        weight_scales = []
+        with tc.psum_pool(name="flipped", bufs=2) as flipped:
+            sym = keep.tile([P, PACK, PACK, P], F32)
+            grad_cols = grad_rows[:].rearrange("p a (s t) -> p a t s", t=PACK)
+            for t in range(PACK):
+                grad_flipped = flipped.tile([P, PACK, P], BF16)
+                for a in range(PACK):
+                    nc.tensor.transpose(grad_flipped[:, a, :], grad_cols[:, a, t, :], ident_bf16[:])
+                nc.vector.tensor_tensor(
+                    out=sym[:, t, :, :],
+                    in0=grad_rows[:, t, :].rearrange("p (m a) -> p a m", a=PACK),
+                    in1=grad_flipped[:],
+                    op=ADD,
+                )
+
+            for part, factor in enumerate((2.0, -2.0)):
+                weights = keep.tile([P, PACK, P, PACK], BF16, name="weights_%d" % part, align_bytes=64)
+                gram_cols = gram_rows[part][:].rearrange("p a (s t) -> p a t s", t=PACK)
+                for a in range(PACK):
+                    gram_flipped = flipped.tile([P, PACK, P], F32)
+                    for t in range(PACK):
+                        nc.tensor.transpose(gram_flipped[:, t, :], gram_cols[:, a, t, :], ident_f32[:])
+                    nc.vector.scalar_tensor_tensor(
+                        out=weights[:, a, :, :],
+                        in0=sym[:, :, a, :].rearrange("p t m -> p m t"),
+                        scalar=factor,
+                        in1=gram_flipped[:].rearrange("p t m -> p m t"),
+                        op0=MULT,
+                        op1=MULT,
+                    )
+                codes = keep.tile([P, STATES], U32, name="weight_codes_%d" % part, align_bytes=64)
+                scales = keep.tile([P, STATES], U8, name="weight_scales_%d" % part, align_bytes=64)
+                nc.vector.quantize_mx(
+                    out=codes[:].bitcast(E5M2_X4),
+                    scales=scales[:],
+                    in_=weights[:].rearrange("p a m t -> p (a m t)"),
+                )
+                weight_codes.append(codes)
+                weight_scales.append(scales)
+
+        sums = stack.enter_context(tc.psum_pool(name="sums", bufs=8))
+        out_rows = out.rearrange("(m a) d -> m a d", a=PACK)
+
+        def regroup(n):
+            grouped = stage.tile([P, 2, N_TILE, PACK], BF16, align_bytes=64)
+            chunk, first = divmod(n * N_TILE, LOAD_COLS)
+            split = N_TILE - SCALAR_COLS
+            for part in range(2):
+                rows = latent_rows[part][chunk][:, :, first : first + N_TILE]
+                nc.vector.tensor_copy(
+                    out=grouped[:, part, :split, :].rearrange("p (c i) t -> p c t i", i=RUN),
+                    in_=rows[:, :, :split].rearrange("p t (c i) -> p c t i", i=RUN),
+                )
+                nc.scalar.copy(
+                    out=grouped[:, part, split:, :].rearrange("p (c i) t -> p c t i", i=RUN),
+                    in_=rows[:, :, split:].rearrange("p t (c i) -> p c t i", i=RUN),
+                )
+            return grouped
+
+        def multiply(n, grouped, result):
+            codes = stage.tile([P, 2 * N_TILE], U32, align_bytes=64)
+            scales = stage.tile([P, 2 * N_TILE], U8, align_bytes=64)
+            nc.vector.quantize_mx(
+                out=codes[:].bitcast(E4M3_X4),
+                scales=scales[:],
+                in_=grouped[:].rearrange("p s w t -> p (s w t)"),
+            )
+            first = (n * N_TILE) % STORE_COLS
+            for a in range(PACK):
+                acc = sums.tile([P, N_TILE], F32)
+                for part in range(2):
+                    tile_rows = slice(a * P, (a + 1) * P)
+                    tile_cols = slice(part * N_TILE, (part + 1) * N_TILE)
+                    nc.tensor.matmul_mx(
+                        out=acc[:],
+                        lhsT=weight_codes[part][:, tile_rows].bitcast(E5M2_X4),
+                        lhsT_scale=weight_scales[part][:, tile_rows],
+                        rhs=codes[:, tile_cols].bitcast(E4M3_X4),
+                        rhs_scale=scales[:, tile_cols],
+                        start=(part == 0),
+                        stop=(part == 1),
+                    )
+                nc.scalar.copy(out=result[:, a, first : first + N_TILE], in_=acc[:])
+
+        n_tiles = DIM // N_TILE
+        tiles_per_store = STORE_COLS // N_TILE
+        grouped_next = regroup(0)
+        result = None
+        for n in range(n_tiles):
+            grouped_now = grouped_next
+            if n + 1 < n_tiles:
+                grouped_next = regroup(n + 1)
+            if n % tiles_per_store == 0:
+                result = results.tile([P, PACK, STORE_COLS], F32, name="result")
+            multiply(n, grouped_now, result)
+            if n % tiles_per_store == tiles_per_store - 1:
+                last = (n + 1) * N_TILE
+                nc.sync.dma_start(out=out_rows[:, :, last - STORE_COLS : last], in_=result[:])

@@ -17,10 +17,10 @@ PACK = 4
 STATES = P * PACK
 DIM = 4096
 N_TILE = 512
+N_TILES = DIM // N_TILE
 LOAD_COLS = 1024
-STORE_COLS = 1024
 RUN = 4
-SCALAR_COLS = 128
+PSUM_BANKS = 8
 
 FLOPS = 2 * 2 * STATES * STATES * DIM
 
@@ -30,19 +30,14 @@ def tile_quantumgraphneuralnetwork_pa_v_kernel(
 ):
     nc = tc.nc
     with ExitStack() as stack:
+        stack.enter_context(tc.manual_schedule())
         keep = stack.enter_context(tc.tile_pool(name="keep", bufs=1))
-        stage = stack.enter_context(tc.tile_pool(name="stage", bufs=3))
-        results = stack.enter_context(tc.tile_pool(name="results", bufs=4))
+        stage = stack.enter_context(tc.tile_pool(name="stage", bufs=4))
+        results = stack.enter_context(tc.tile_pool(name="results", bufs=N_TILES))
 
-        grad_rows = keep.tile([P, PACK, STATES], BF16)
-        nc.sync.dma_start(out=grad_rows[:], in_=grad_out.rearrange("(p r) c -> p r c", r=PACK))
-        gram_rows = []
-        for part, gram in enumerate((g_re, g_im)):
-            rows = keep.tile([P, PACK, STATES], F32, name="gram_rows_%d" % part)
-            nc.sync.dma_start(out=rows[:], in_=gram.rearrange("(p r) c -> p r c", r=PACK))
-            gram_rows.append(rows)
         latent_rows = [[], []]
-        for chunk in range(DIM // LOAD_COLS):
+
+        def load_latents(chunk):
             cols = slice(chunk * LOAD_COLS, (chunk + 1) * LOAD_COLS)
             for part, latent in enumerate((latent_re, latent_im)):
                 rows = keep.tile([P, PACK, LOAD_COLS], BF16, name="latent_rows_%d_%d" % (part, chunk))
@@ -51,14 +46,72 @@ def tile_quantumgraphneuralnetwork_pa_v_kernel(
                 )
                 latent_rows[part].append(rows)
 
+        grad_rows = keep.tile([P, PACK, STATES], BF16)
+        nc.sync.dma_start(out=grad_rows[:], in_=grad_out.rearrange("(p r) c -> p r c", r=PACK))
+        load_latents(0)
+        gram_rows = []
+        for part, gram in enumerate((g_re, g_im)):
+            rows = keep.tile([P, PACK, STATES], F32, name="gram_rows_%d" % part)
+            nc.sync.dma_start(out=rows[:], in_=gram.rearrange("(p r) c -> p r c", r=PACK))
+            gram_rows.append(rows)
+        for chunk in range(1, DIM // LOAD_COLS):
+            load_latents(chunk)
+
         ident_bf16 = keep.tile([P, P], BF16)
         make_identity(nc, ident_bf16[:])
         ident_f32 = keep.tile([P, P], F32)
         make_identity(nc, ident_f32[:])
 
+        grouped_tiles = {}
+        latent_codes = {}
+        latent_scales = {}
+
+        def regroup(n, copy):
+            grouped = stage.tile([P, 2, N_TILE, PACK], BF16, align_bytes=64)
+            chunk, first = divmod(n * N_TILE, LOAD_COLS)
+            for part in range(2):
+                rows = latent_rows[part][chunk][:, :, first : first + N_TILE]
+                copy(
+                    out=grouped[:, part, :, :].rearrange("p (c i) t -> p c t i", i=RUN),
+                    in_=rows.rearrange("p t (c i) -> p c t i", i=RUN),
+                )
+            grouped_tiles[n] = grouped
+
+        def quantise(n):
+            codes = stage.tile([P, 2 * N_TILE], U32, align_bytes=64)
+            scales = stage.tile([P, 2 * N_TILE], U8, align_bytes=64)
+            nc.vector.quantize_mx(
+                out=codes[:].bitcast(E4M3_X4),
+                scales=scales[:],
+                in_=grouped_tiles[n][:].rearrange("p s w t -> p (s w t)"),
+            )
+            latent_codes[n] = codes
+            latent_scales[n] = scales
+
+        def multiply(n, sums):
+            result = results.tile([P, PACK, N_TILE], F32)
+            for a in range(PACK):
+                acc = sums.tile([P, N_TILE], F32)
+                for part in range(2):
+                    tile_rows = slice(a * P, (a + 1) * P)
+                    tile_cols = slice(part * N_TILE, (part + 1) * N_TILE)
+                    nc.tensor.matmul_mx(
+                        out=acc[:],
+                        lhsT=weight_codes[part][:, tile_rows].bitcast(E5M2_X4),
+                        lhsT_scale=weight_scales[part][:, tile_rows],
+                        rhs=latent_codes[n][:, tile_cols].bitcast(E4M3_X4),
+                        rhs_scale=latent_scales[n][:, tile_cols],
+                        start=(part == 0),
+                        stop=(part == 1),
+                    )
+                nc.scalar.copy(out=result[:, a, :], in_=acc[:])
+                nc.sync.dma_start(
+                    out=out_rows[:, a, n * N_TILE : (n + 1) * N_TILE], in_=result[:, a, :]
+                )
+
         weight_codes = []
         weight_scales = []
-        with tc.psum_pool(name="flipped", bufs=2) as flipped:
+        with tc.psum_pool(name="flipped", bufs=PSUM_BANKS // 2) as flipped:
             sym = keep.tile([P, PACK, PACK, P], F32)
             grad_cols = grad_rows[:].rearrange("p a (s t) -> p a t s", t=PACK)
             for t in range(PACK):
@@ -71,6 +124,10 @@ def tile_quantumgraphneuralnetwork_pa_v_kernel(
                     in1=grad_flipped[:],
                     op=ADD,
                 )
+
+            regroup(0, nc.scalar.copy)
+            regroup(1, nc.vector.tensor_copy)
+            quantise(0)
 
             for part, factor in enumerate((2.0, -2.0)):
                 weights = keep.tile([P, PACK, P, PACK], BF16, name="weights_%d" % part, align_bytes=64)
@@ -97,61 +154,13 @@ def tile_quantumgraphneuralnetwork_pa_v_kernel(
                 weight_codes.append(codes)
                 weight_scales.append(scales)
 
-        sums = stack.enter_context(tc.psum_pool(name="sums", bufs=8))
+        regroup(2, nc.scalar.copy)
+
         out_rows = out.rearrange("(m a) d -> m a d", a=PACK)
-
-        def regroup(n):
-            grouped = stage.tile([P, 2, N_TILE, PACK], BF16, align_bytes=64)
-            chunk, first = divmod(n * N_TILE, LOAD_COLS)
-            split = N_TILE - SCALAR_COLS
-            for part in range(2):
-                rows = latent_rows[part][chunk][:, :, first : first + N_TILE]
-                nc.vector.tensor_copy(
-                    out=grouped[:, part, :split, :].rearrange("p (c i) t -> p c t i", i=RUN),
-                    in_=rows[:, :, :split].rearrange("p t (c i) -> p c t i", i=RUN),
-                )
-                nc.scalar.copy(
-                    out=grouped[:, part, split:, :].rearrange("p (c i) t -> p c t i", i=RUN),
-                    in_=rows[:, :, split:].rearrange("p t (c i) -> p c t i", i=RUN),
-                )
-            return grouped
-
-        def multiply(n, grouped, result):
-            codes = stage.tile([P, 2 * N_TILE], U32, align_bytes=64)
-            scales = stage.tile([P, 2 * N_TILE], U8, align_bytes=64)
-            nc.vector.quantize_mx(
-                out=codes[:].bitcast(E4M3_X4),
-                scales=scales[:],
-                in_=grouped[:].rearrange("p s w t -> p (s w t)"),
-            )
-            first = (n * N_TILE) % STORE_COLS
-            for a in range(PACK):
-                acc = sums.tile([P, N_TILE], F32)
-                for part in range(2):
-                    tile_rows = slice(a * P, (a + 1) * P)
-                    tile_cols = slice(part * N_TILE, (part + 1) * N_TILE)
-                    nc.tensor.matmul_mx(
-                        out=acc[:],
-                        lhsT=weight_codes[part][:, tile_rows].bitcast(E5M2_X4),
-                        lhsT_scale=weight_scales[part][:, tile_rows],
-                        rhs=codes[:, tile_cols].bitcast(E4M3_X4),
-                        rhs_scale=scales[:, tile_cols],
-                        start=(part == 0),
-                        stop=(part == 1),
-                    )
-                nc.scalar.copy(out=result[:, a, first : first + N_TILE], in_=acc[:])
-
-        n_tiles = DIM // N_TILE
-        tiles_per_store = STORE_COLS // N_TILE
-        grouped_next = regroup(0)
-        result = None
-        for n in range(n_tiles):
-            grouped_now = grouped_next
-            if n + 1 < n_tiles:
-                grouped_next = regroup(n + 1)
-            if n % tiles_per_store == 0:
-                result = results.tile([P, PACK, STORE_COLS], F32, name="result")
-            multiply(n, grouped_now, result)
-            if n % tiles_per_store == tiles_per_store - 1:
-                last = (n + 1) * N_TILE
-                nc.sync.dma_start(out=out_rows[:, :, last - STORE_COLS : last], in_=result[:])
+        sums = stack.enter_context(tc.psum_pool(name="sums", bufs=PSUM_BANKS))
+        for n in range(N_TILES):
+            multiply(n, sums)
+            if n + 1 < N_TILES:
+                quantise(n + 1)
+            if n + 3 < N_TILES:
+                regroup(n + 3, nc.vector.tensor_copy)

@@ -36,26 +36,27 @@ def tile_quantumgraphneuralnetwork_pa_v_kernel(
         results = stack.enter_context(tc.tile_pool(name="results", bufs=N_TILES))
 
         latent_rows = [[], []]
+        latents = (latent_re, latent_im)
 
-        def load_latents(chunk):
+        def load_latent(part, chunk):
             cols = slice(chunk * LOAD_COLS, (chunk + 1) * LOAD_COLS)
-            for part, latent in enumerate((latent_re, latent_im)):
-                rows = keep.tile([P, PACK, LOAD_COLS], BF16, name="latent_rows_%d_%d" % (part, chunk))
-                nc.sync.dma_start(
-                    out=rows[:], in_=latent.rearrange("(p t) d -> p t d", t=PACK)[:, :, cols]
-                )
-                latent_rows[part].append(rows)
+            rows = keep.tile([P, PACK, LOAD_COLS], BF16, name="latent_rows_%d_%d" % (part, chunk))
+            nc.sync.dma_start(
+                out=rows[:], in_=latents[part].rearrange("(p t) d -> p t d", t=PACK)[:, :, cols]
+            )
+            latent_rows[part].append(rows)
 
         grad_rows = keep.tile([P, PACK, STATES], BF16)
         nc.sync.dma_start(out=grad_rows[:], in_=grad_out.rearrange("(p r) c -> p r c", r=PACK))
-        load_latents(0)
         gram_rows = []
         for part, gram in enumerate((g_re, g_im)):
+            load_latent(part, 0)
             rows = keep.tile([P, PACK, STATES], F32, name="gram_rows_%d" % part)
             nc.sync.dma_start(out=rows[:], in_=gram.rearrange("(p r) c -> p r c", r=PACK))
             gram_rows.append(rows)
         for chunk in range(1, DIM // LOAD_COLS):
-            load_latents(chunk)
+            for part in range(2):
+                load_latent(part, chunk)
 
         ident_bf16 = keep.tile([P, P], BF16)
         make_identity(nc, ident_bf16[:])
@@ -66,16 +67,15 @@ def tile_quantumgraphneuralnetwork_pa_v_kernel(
         latent_codes = {}
         latent_scales = {}
 
-        def regroup(n, copy):
-            grouped = stage.tile([P, 2, N_TILE, PACK], BF16, align_bytes=64)
+        def regroup(n, part, copy):
+            if part == 0:
+                grouped_tiles[n] = stage.tile([P, 2, N_TILE, PACK], BF16, name="grouped", align_bytes=64)
             chunk, first = divmod(n * N_TILE, LOAD_COLS)
-            for part in range(2):
-                rows = latent_rows[part][chunk][:, :, first : first + N_TILE]
-                copy(
-                    out=grouped[:, part, :, :].rearrange("p (c i) t -> p c t i", i=RUN),
-                    in_=rows.rearrange("p t (c i) -> p c t i", i=RUN),
-                )
-            grouped_tiles[n] = grouped
+            rows = latent_rows[part][chunk][:, :, first : first + N_TILE]
+            copy(
+                out=grouped_tiles[n][:, part, :, :].rearrange("p (c i) t -> p c t i", i=RUN),
+                in_=rows.rearrange("p t (c i) -> p c t i", i=RUN),
+            )
 
         def quantise(n):
             codes = stage.tile([P, 2 * N_TILE], U32, align_bytes=64)
@@ -125,11 +125,7 @@ def tile_quantumgraphneuralnetwork_pa_v_kernel(
                     op=ADD,
                 )
 
-            regroup(0, nc.scalar.copy)
-            regroup(1, nc.vector.tensor_copy)
-            quantise(0)
-
-            for part, factor in enumerate((2.0, -2.0)):
+            def build_weights(part, factor):
                 weights = keep.tile([P, PACK, P, PACK], BF16, name="weights_%d" % part, align_bytes=64)
                 gram_cols = gram_rows[part][:].rearrange("p a (s t) -> p a t s", t=PACK)
                 for a in range(PACK):
@@ -154,7 +150,17 @@ def tile_quantumgraphneuralnetwork_pa_v_kernel(
                 weight_codes.append(codes)
                 weight_scales.append(scales)
 
-        regroup(2, nc.scalar.copy)
+            tiles_per_load = LOAD_COLS // N_TILE
+            for n in range(tiles_per_load):
+                regroup(n, 0, nc.scalar.copy)
+            build_weights(0, 2.0)
+            for n in range(tiles_per_load):
+                regroup(n, 1, nc.scalar.copy)
+            quantise(0)
+            build_weights(1, -2.0)
+            for part in range(2):
+                regroup(tiles_per_load, part, nc.scalar.copy)
+        first_by_vector = tiles_per_load + 1
 
         out_rows = out.rearrange("(m a) d -> m a d", a=PACK)
         sums = stack.enter_context(tc.psum_pool(name="sums", bufs=PSUM_BANKS))
@@ -162,5 +168,6 @@ def tile_quantumgraphneuralnetwork_pa_v_kernel(
             multiply(n, sums)
             if n + 1 < N_TILES:
                 quantise(n + 1)
-            if n + 3 < N_TILES:
-                regroup(n + 3, nc.vector.tensor_copy)
+            if n + first_by_vector < N_TILES:
+                for part in range(2):
+                    regroup(n + first_by_vector, part, nc.vector.tensor_copy)

@@ -21,6 +21,7 @@ N_TILES = DIM // N_TILE
 LOAD_COLS = 1024
 RUN = 4
 PSUM_BANKS = 8
+PAIRED_TILES = 6
 
 FLOPS = 2 * 2 * STATES * STATES * DIM
 
@@ -33,7 +34,7 @@ def tile_quantumgraphneuralnetwork_pa_v_kernel(
         stack.enter_context(tc.manual_schedule())
         keep = stack.enter_context(tc.tile_pool(name="keep", bufs=1))
         stage = stack.enter_context(tc.tile_pool(name="stage", bufs=4))
-        results = stack.enter_context(tc.tile_pool(name="results", bufs=N_TILES))
+        results = stack.enter_context(tc.tile_pool(name="results", bufs=N_TILES // 2))
 
         latent_rows = [[], []]
         latents = (latent_re, latent_im)
@@ -66,6 +67,7 @@ def tile_quantumgraphneuralnetwork_pa_v_kernel(
         grouped_tiles = {}
         latent_codes = {}
         latent_scales = {}
+        result_pairs = {}
 
         def regroup(n, part, copy):
             if part == 0:
@@ -89,7 +91,11 @@ def tile_quantumgraphneuralnetwork_pa_v_kernel(
             latent_scales[n] = scales
 
         def multiply(n, sums):
-            result = results.tile([P, PACK, N_TILE], F32)
+            half = n % 2
+            if half == 0:
+                result_pairs[n // 2] = results.tile([P, PACK, 2 * N_TILE], F32, name="result")
+            result = result_pairs[n // 2]
+            half_cols = slice(half * N_TILE, (half + 1) * N_TILE)
             for a in range(PACK):
                 acc = sums.tile([P, N_TILE], F32)
                 for part in range(2):
@@ -104,10 +110,15 @@ def tile_quantumgraphneuralnetwork_pa_v_kernel(
                         start=(part == 0),
                         stop=(part == 1),
                     )
-                nc.scalar.copy(out=result[:, a, :], in_=acc[:])
-                nc.sync.dma_start(
-                    out=out_rows[:, a, n * N_TILE : (n + 1) * N_TILE], in_=result[:, a, :]
-                )
+                nc.scalar.copy(out=result[:, a, half_cols], in_=acc[:])
+                if n >= PAIRED_TILES:
+                    nc.sync.dma_start(
+                        out=out_rows[:, a, n * N_TILE : (n + 1) * N_TILE], in_=result[:, a, half_cols]
+                    )
+                elif half == 1:
+                    nc.sync.dma_start(
+                        out=out_rows[:, a, (n - 1) * N_TILE : (n + 1) * N_TILE], in_=result[:, a, :]
+                    )
 
         weight_codes = []
         weight_scales = []

from contextlib import ExitStack

import concourse.mybir as mybir
from concourse.masks import make_identity

F32 = mybir.dt.float32
BF16 = mybir.dt.bfloat16
U32 = mybir.dt.uint32
U8 = mybir.dt.uint8
E4M3_X4 = mybir.dt.float8_e4m3fn_x4
E5M2_X4 = mybir.dt.float8_e5m2_x4
ADD = mybir.AluOpType.add
MULT = mybir.AluOpType.mult

P = 128
PACK = 4
STATES = P * PACK
DIM = 4096
N_TILE = 512
N_TILES = DIM // N_TILE
LOAD_COLS = 1024
RUN = 4
PSUM_BANKS = 8
PAIRED_TILES = 6

FLOPS = 2 * 2 * STATES * STATES * DIM


def tile_quantumgraphneuralnetwork_pa_v_kernel(
    tc, latent_re, latent_im, g_re, g_im, grad_out, out
):
    nc = tc.nc
    with ExitStack() as stack:
        stack.enter_context(tc.manual_schedule())
        keep = stack.enter_context(tc.tile_pool(name="keep", bufs=1))
        stage = stack.enter_context(tc.tile_pool(name="stage", bufs=4))
        results = stack.enter_context(tc.tile_pool(name="results", bufs=N_TILES // 2))

        latent_rows = [[], []]
        latents = (latent_re, latent_im)

        def load_latent(part, chunk):
            cols = slice(chunk * LOAD_COLS, (chunk + 1) * LOAD_COLS)
            rows = keep.tile([P, PACK, LOAD_COLS], BF16, name="latent_rows_%d_%d" % (part, chunk))
            nc.sync.dma_start(
                out=rows[:], in_=latents[part].rearrange("(p t) d -> p t d", t=PACK)[:, :, cols]
            )
            latent_rows[part].append(rows)

        grad_rows = keep.tile([P, PACK, STATES], BF16)
        nc.sync.dma_start(out=grad_rows[:], in_=grad_out.rearrange("(p r) c -> p r c", r=PACK))
        gram_rows = []
        for part, gram in enumerate((g_re, g_im)):
            load_latent(part, 0)
            rows = keep.tile([P, PACK, STATES], F32, name="gram_rows_%d" % part)
            nc.sync.dma_start(out=rows[:], in_=gram.rearrange("(p r) c -> p r c", r=PACK))
            gram_rows.append(rows)
        for chunk in range(1, DIM // LOAD_COLS):
            for part in range(2):
                load_latent(part, chunk)

        ident_bf16 = keep.tile([P, P], BF16)
        make_identity(nc, ident_bf16[:])
        ident_f32 = keep.tile([P, P], F32)
        make_identity(nc, ident_f32[:])

        grouped_tiles = {}
        latent_codes = {}
        latent_scales = {}
        result_pairs = {}

        def regroup(n, part, copy):
            if part == 0:
                grouped_tiles[n] = stage.tile([P, 2, N_TILE, PACK], BF16, name="grouped", align_bytes=64)
            chunk, first = divmod(n * N_TILE, LOAD_COLS)
            rows = latent_rows[part][chunk][:, :, first : first + N_TILE]
            copy(
                out=grouped_tiles[n][:, part, :, :].rearrange("p (c i) t -> p c t i", i=RUN),
                in_=rows.rearrange("p t (c i) -> p c t i", i=RUN),
            )

        def quantise(n):
            codes = stage.tile([P, 2 * N_TILE], U32, align_bytes=64)
            scales = stage.tile([P, 2 * N_TILE], U8, align_bytes=64)
            nc.vector.quantize_mx(
                out=codes[:].bitcast(E4M3_X4),
                scales=scales[:],
                in_=grouped_tiles[n][:].rearrange("p s w t -> p (s w t)"),
            )
            latent_codes[n] = codes
            latent_scales[n] = scales

        def multiply(n, sums):
            half = n % 2
            if half == 0:
                result_pairs[n // 2] = results.tile([P, PACK, 2 * N_TILE], F32, name="result")
            result = result_pairs[n // 2]
            half_cols = slice(half * N_TILE, (half + 1) * N_TILE)
            for a in range(PACK):
                acc = sums.tile([P, N_TILE], F32)
                for part in range(2):
                    tile_rows = slice(a * P, (a + 1) * P)
                    tile_cols = slice(part * N_TILE, (part + 1) * N_TILE)
                    nc.tensor.matmul_mx(
                        out=acc[:],
                        lhsT=weight_codes[part][:, tile_rows].bitcast(E5M2_X4),
                        lhsT_scale=weight_scales[part][:, tile_rows],
                        rhs=latent_codes[n][:, tile_cols].bitcast(E4M3_X4),
                        rhs_scale=latent_scales[n][:, tile_cols],
                        start=(part == 0),
                        stop=(part == 1),
                    )
                nc.scalar.copy(out=result[:, a, half_cols], in_=acc[:])
                if n >= PAIRED_TILES:
                    nc.sync.dma_start(
                        out=out_rows[:, a, n * N_TILE : (n + 1) * N_TILE], in_=result[:, a, half_cols]
                    )
                elif half == 1:
                    nc.sync.dma_start(
                        out=out_rows[:, a, (n - 1) * N_TILE : (n + 1) * N_TILE], in_=result[:, a, :]
                    )

        weight_codes = []
        weight_scales = []
        with tc.psum_pool(name="flipped", bufs=PSUM_BANKS // 2) as flipped:
            sym = keep.tile([P, PACK, PACK, P], F32)
            grad_cols = grad_rows[:].rearrange("p a (s t) -> p a t s", t=PACK)
            for t in range(PACK):
                grad_flipped = flipped.tile([P, PACK, P], BF16)
                for a in range(PACK):
                    nc.tensor.transpose(grad_flipped[:, a, :], grad_cols[:, a, t, :], ident_bf16[:])
                nc.vector.tensor_tensor(
                    out=sym[:, t, :, :],
                    in0=grad_rows[:, t, :].rearrange("p (m a) -> p a m", a=PACK),
                    in1=grad_flipped[:],
                    op=ADD,
                )

            def build_weights(part, factor):
                weights = keep.tile([P, PACK, P, PACK], BF16, name="weights_%d" % part, align_bytes=64)
                gram_cols = gram_rows[part][:].rearrange("p a (s t) -> p a t s", t=PACK)
                for a in range(PACK):
                    gram_flipped = flipped.tile([P, PACK, P], F32)
                    for t in range(PACK):
                        nc.tensor.transpose(gram_flipped[:, t, :], gram_cols[:, a, t, :], ident_f32[:])
                    nc.vector.scalar_tensor_tensor(
                        out=weights[:, a, :, :],
                        in0=sym[:, :, a, :].rearrange("p t m -> p m t"),
                        scalar=factor,
                        in1=gram_flipped[:].rearrange("p t m -> p m t"),
                        op0=MULT,
                        op1=MULT,
                    )
                codes = keep.tile([P, STATES], U32, name="weight_codes_%d" % part, align_bytes=64)
                scales = keep.tile([P, STATES], U8, name="weight_scales_%d" % part, align_bytes=64)
                nc.vector.quantize_mx(
                    out=codes[:].bitcast(E5M2_X4),
                    scales=scales[:],
                    in_=weights[:].rearrange("p a m t -> p (a m t)"),
                )
                weight_codes.append(codes)
                weight_scales.append(scales)

            tiles_per_load = LOAD_COLS // N_TILE
            for n in range(tiles_per_load):
                regroup(n, 0, nc.scalar.copy)
            build_weights(0, 2.0)
            for n in range(tiles_per_load):
                regroup(n, 1, nc.scalar.copy)
            quantise(0)
            build_weights(1, -2.0)
            for part in range(2):
                regroup(tiles_per_load, part, nc.scalar.copy)
        first_by_vector = tiles_per_load + 1

        out_rows = out.rearrange("(m a) d -> m a d", a=PACK)
        sums = stack.enter_context(tc.psum_pool(name="sums", bufs=PSUM_BANKS))
        for n in range(N_TILES):
            multiply(n, sums)
            if n + 1 < N_TILES:
                quantise(n + 1)
            if n + first_by_vector < N_TILES:
                for part in range(2):
                    regroup(n + first_by_vector, part, nc.vector.tensor_copy)
